import numpy as np
import ml_dtypes

BF16 = ml_dtypes.bfloat16


def bf(x):
    return np.asarray(x, np.float32).astype(BF16)


def f32(x):
    return np.asarray(x, np.float32)


def f64(x):
    return np.asarray(x).astype(np.float64)


def striped(idx):
    return np.tile(idx.reshape(-1, 16).T, (8, 1))


C, I, S, N = 256, 512, 256, 128
EPS = 1e-6


def silu(v):
    return v / (1.0 + np.exp(-v))


def setup_inputs():
    return {"base": f32(np.random.standard_normal((C, S))), "x": f32(np.random.standard_normal((C, N))), "gain": f32(1.0 + 0.1 * np.random.standard_normal((C, 1))), "w1": bf(np.random.standard_normal((C, I)) / np.sqrt(C)), "w2": bf(np.random.standard_normal((I, C)) / np.sqrt(I)), "offs": striped(np.random.permutation(S)[:N])}


def reference(base, x, gain, w1, w2, offs):
    idx = offs[:16].T.reshape(-1)
    xs = f64(x)
    r = 1.0 / np.sqrt(np.mean(xs * xs, axis=0, keepdims=True) + EPS)
    h = f64(gain) * xs * r
    u = silu(f64(w1).T @ h)
    y = f64(w2).T @ u
    out = f64(base).copy()
    out[:, idx] = xs + y
    return out

@@ -1,0 +1,80 @@
+import concourse.mybir as mybir
+
+P = 128
+C, I, S, N = 256, 512, 256, 128
+CB = C // P
+EB = I // P
+EPS = 1e-6
+FLOPS = 4 * C * I * N
+
+F32, BF16, U16 = mybir.dt.float32, mybir.dt.bfloat16, mybir.dt.uint16
+MULT, ADD = mybir.AluOpType.mult, mybir.AluOpType.add
+ACT = mybir.ActivationFunctionType
+
+
+def tile_thinkerdecoderlayer_kernel(tc, base, x, gain, w1, w2, offs, out):
+    nc = tc.nc
+    with (
+        tc.tile_pool(name="held", bufs=1) as held,
+        tc.psum_pool(name="psum", bufs=1) as psum,
+    ):
+        offsets = held.tile([P, N // 16], U16, name="offsets")
+        x_sb = [held.tile([P, N], F32, name=f"x{c}") for c in range(CB)]
+        gain_sb = [held.tile([P, 1], F32, name=f"gain{c}") for c in range(CB)]
+        w1_sb = [held.tile([P, I], BF16, name=f"w1_{c}") for c in range(CB)]
+        w2_sb = [held.tile([P, C], BF16, name=f"w2_{e}") for e in range(EB)]
+        window = [held.tile([P, S], F32, name=f"window{c}") for c in range(CB)]
+
+        for c in range(CB):
+            nc.sync.dma_start(x_sb[c][:], x[c * P : (c + 1) * P, :])
+        for c in range(CB):
+            nc.scalar.dma_start(gain_sb[c][:], gain[c * P : (c + 1) * P, :])
+        for c in range(CB):
+            nc.scalar.dma_start(w1_sb[c][:], w1[c * P : (c + 1) * P, :])
+        for e in range(EB):
+            nc.gpsimd.dma_start(w2_sb[e][:], w2[e * P : (e + 1) * P, :])
+        nc.sync.dma_start(offsets[:], offs)
+        for c in range(CB):
+            nc.sync.dma_start(window[c][:], base[c * P : (c + 1) * P, :])
+
+        averager = held.tile([P, P], F32, name="averager")
+        nc.vector.memset(averager[:], 1.0 / C)
+        eps = held.tile([P, 1], F32, name="eps")
+        nc.vector.memset(eps[:], EPS)
+
+        mean_sq = psum.tile([P, N], F32, name="mean_sq")
+        for c in range(CB):
+            x_sq = held.tile([P, N], F32, name=f"x_sq{c}")
+            nc.vector.tensor_tensor(x_sq[:], x_sb[c][:], x_sb[c][:], MULT)
+            nc.tensor.matmul(mean_sq[:], averager[:], x_sq[:], start=(c == 0), stop=(c == CB - 1))
+        r = held.tile([P, N], F32, name="r")
+        nc.scalar.activation(r[:], mean_sq[:], ACT.Abs_reciprocal_sqrt, bias=eps[:])
+
+        h = [held.tile([P, N], BF16, name=f"h{c}") for c in range(CB)]
+        for c in range(CB):
+            nc.vector.scalar_tensor_tensor(h[c][:], x_sb[c][:], gain_sb[c][:], r[:], MULT, MULT)
+
+        pre = [psum.tile([P, N], F32, name=f"pre{e}") for e in range(EB)]
+        for c in range(CB):
+            for e in range(EB):
+                nc.tensor.matmul(
+                    pre[e][:], w1_sb[c][:, e * P : (e + 1) * P], h[c][:],
+                    start=(c == 0), stop=(c == CB - 1),
+                )
+
+        y = [psum.tile([P, N], F32, name=f"y{c}") for c in range(CB)]
+        for e in range(EB):
+            u = held.tile([P, N], BF16, name=f"u{e}")
+            nc.scalar.activation(u[:], pre[e][:], ACT.Silu)
+            for c in range(CB):
+                nc.tensor.matmul(
+                    y[c][:], w2_sb[e][:, c * P : (c + 1) * P], u[:],
+                    start=(e == 0), stop=(e == EB - 1),
+                )
+
+        for c in range(CB):
+            y_sb = held.tile([P, N], F32, name=f"y_sb{c}")
+            nc.scalar.copy(y_sb[:], y[c][:])
+            nc.vector.tensor_tensor(window[c][:].indirect(offsets[:]), x_sb[c][:], y_sb[:], ADD)
+            store = nc.sync if c % 2 == 0 else nc.scalar
+            store.dma_start(out[c * P : (c + 1) * P, :], window[c][:])

@@ -32,7 +32,7 @@ def tile_thinkerdecoderlayer_kernel(tc, base, x, gain, w1, w2, offs, out):
         for c in range(CB):
             nc.scalar.dma_start(w1_sb[c][:], w1[c * P : (c + 1) * P, :])
         for e in range(EB):
-            nc.gpsimd.dma_start(w2_sb[e][:], w2[e * P : (e + 1) * P, :])
+            nc.sync.dma_start(w2_sb[e][:], w2[e * P : (e + 1) * P, :])
         nc.sync.dma_start(offsets[:], offs)
         for c in range(CB):
             nc.sync.dma_start(window[c][:], base[c * P : (c + 1) * P, :])

@@ -6,6 +6,8 @@ CB = C // P
 EB = I // P
 EPS = 1e-6
 FLOPS = 4 * C * I * N
+WARM_COLS = 512
+WARM_MATMULS = 4
 
 F32, BF16, U16 = mybir.dt.float32, mybir.dt.bfloat16, mybir.dt.uint16
 MULT, ADD = mybir.AluOpType.mult, mybir.AluOpType.add
@@ -36,6 +38,12 @@ def tile_thinkerdecoderlayer_kernel(tc, base, x, gain, w1, w2, offs, out):
         nc.sync.dma_start(offsets[:], offs)
         for c in range(CB):
             nc.sync.dma_start(window[c][:], base[c * P : (c + 1) * P, :])
+
+        zeros = held.tile([P, WARM_COLS], BF16, name="zeros")
+        nc.vector.memset(zeros[:], 0.0)
+        unread = psum.tile([P, WARM_COLS], F32, name="unread")
+        for i in range(WARM_MATMULS):
+            nc.tensor.matmul(unread[:], zeros[:, 0:P], zeros[:], start=True, stop=True)
 
         averager = held.tile([P, P], F32, name="averager")
         nc.vector.memset(averager[:], 1.0 / C)

@@ -6,8 +6,7 @@ CB = C // P
 EB = I // P
 EPS = 1e-6
 FLOPS = 4 * C * I * N
-WARM_COLS = 512
-WARM_MATMULS = 4
+WARM_MATMULS = 3
 
 F32, BF16, U16 = mybir.dt.float32, mybir.dt.bfloat16, mybir.dt.uint16
 MULT, ADD = mybir.AluOpType.mult, mybir.AluOpType.add
@@ -39,16 +38,14 @@ def tile_thinkerdecoderlayer_kernel(tc, base, x, gain, w1, w2, offs, out):
         for c in range(CB):
             nc.sync.dma_start(window[c][:], base[c * P : (c + 1) * P, :])
 
-        zeros = held.tile([P, WARM_COLS], BF16, name="zeros")
-        nc.vector.memset(zeros[:], 0.0)
-        unread = psum.tile([P, WARM_COLS], F32, name="unread")
-        for i in range(WARM_MATMULS):
-            nc.tensor.matmul(unread[:], zeros[:, 0:P], zeros[:], start=True, stop=True)
-
         averager = held.tile([P, P], F32, name="averager")
         nc.vector.memset(averager[:], 1.0 / C)
         eps = held.tile([P, 1], F32, name="eps")
         nc.vector.memset(eps[:], EPS)
+
+        unread = psum.tile([P, P], F32, name="unread")
+        for i in range(WARM_MATMULS):
+            nc.tensor.matmul(unread[:], averager[:], averager[:], start=True, stop=True)
 
         mean_sq = psum.tile([P, N], F32, name="mean_sq")
         for c in range(CB):

@@ -81,5 +81,5 @@ def tile_thinkerdecoderlayer_kernel(tc, base, x, gain, w1, w2, offs, out):
             y_sb = held.tile([P, N], F32, name=f"y_sb{c}")
             nc.scalar.copy(y_sb[:], y[c][:])
             nc.vector.tensor_tensor(window[c][:].indirect(offsets[:]), x_sb[c][:], y_sb[:], ADD)
-            store = nc.sync if c % 2 == 0 else nc.scalar
+            store = nc.scalar if c % 2 == 0 else nc.sync
             store.dma_start(out[c * P : (c + 1) * P, :], window[c][:])

@@ -7,6 +7,7 @@ EB = I // P
 EPS = 1e-6
 FLOPS = 4 * C * I * N
 WARM_MATMULS = 3
+WARM_COLUMNS = 32
 
 F32, BF16, U16 = mybir.dt.float32, mybir.dt.bfloat16, mybir.dt.uint16
 MULT, ADD = mybir.AluOpType.mult, mybir.AluOpType.add
@@ -43,9 +44,9 @@ def tile_thinkerdecoderlayer_kernel(tc, base, x, gain, w1, w2, offs, out):
         eps = held.tile([P, 1], F32, name="eps")
         nc.vector.memset(eps[:], EPS)
 
-        unread = psum.tile([P, P], F32, name="unread")
+        unread = psum.tile([WARM_COLUMNS, P], F32, name="unread")
         for i in range(WARM_MATMULS):
-            nc.tensor.matmul(unread[:], averager[:], averager[:], start=True, stop=True)
+            nc.tensor.matmul(unread[:], averager[:, 0:WARM_COLUMNS], averager[:], start=True, stop=True)
 
         mean_sq = psum.tile([P, N], F32, name="mean_sq")
         for c in range(CB):

@@ -41,8 +41,6 @@ def tile_thinkerdecoderlayer_kernel(tc, base, x, gain, w1, w2, offs, out):
 
         averager = held.tile([P, P], F32, name="averager")
         nc.vector.memset(averager[:], 1.0 / C)
-        eps = held.tile([P, 1], F32, name="eps")
-        nc.vector.memset(eps[:], EPS)
 
         unread = psum.tile([WARM_COLUMNS, P], F32, name="unread")
         for i in range(WARM_MATMULS):
@@ -54,7 +52,7 @@ def tile_thinkerdecoderlayer_kernel(tc, base, x, gain, w1, w2, offs, out):
             nc.vector.tensor_tensor(x_sq[:], x_sb[c][:], x_sb[c][:], MULT)
             nc.tensor.matmul(mean_sq[:], averager[:], x_sq[:], start=(c == 0), stop=(c == CB - 1))
         r = held.tile([P, N], F32, name="r")
-        nc.scalar.activation(r[:], mean_sq[:], ACT.Abs_reciprocal_sqrt, bias=eps[:])
+        nc.scalar.activation(r[:], mean_sq[:], ACT.Abs_reciprocal_sqrt, bias=EPS)
 
         h = [held.tile([P, N], BF16, name=f"h{c}") for c in range(CB)]
         for c in range(CB):
@@ -69,18 +67,22 @@ def tile_thinkerdecoderlayer_kernel(tc, base, x, gain, w1, w2, offs, out):
                 )
 
         y = [psum.tile([P, N], F32, name=f"y{c}") for c in range(CB)]
+        u = [held.tile([P, N], BF16, name=f"u{e}") for e in range(EB)]
         for e in range(EB):
-            u = held.tile([P, N], BF16, name=f"u{e}")
-            nc.scalar.activation(u[:], pre[e][:], ACT.Silu)
-            for c in range(CB):
+            nc.scalar.activation(u[e][:], pre[e][:], ACT.Silu)
+        for c in range(CB):
+            for e in range(EB):
                 nc.tensor.matmul(
-                    y[c][:], w2_sb[e][:, c * P : (c + 1) * P], u[:],
+                    y[c][:], w2_sb[e][:, c * P : (c + 1) * P], u[e][:],
                     start=(e == 0), stop=(e == EB - 1),
                 )
 
         for c in range(CB):
             y_sb = held.tile([P, N], F32, name=f"y_sb{c}")
-            nc.scalar.copy(y_sb[:], y[c][:])
+            if c == 0:
+                nc.vector.tensor_copy(y_sb[:], y[c][:])
+            else:
+                nc.scalar.copy(y_sb[:], y[c][:])
             nc.vector.tensor_tensor(window[c][:].indirect(offsets[:]), x_sb[c][:], y_sb[:], ADD)
             store = nc.scalar if c % 2 == 0 else nc.sync
             store.dma_start(out[c * P : (c + 1) * P, :], window[c][:])

import concourse.mybir as mybir

P = 128
C, I, S, N = 256, 512, 256, 128
CB = C // P
EB = I // P
EPS = 1e-6
FLOPS = 4 * C * I * N
WARM_MATMULS = 3
WARM_COLUMNS = 32

F32, BF16, U16 = mybir.dt.float32, mybir.dt.bfloat16, mybir.dt.uint16
MULT, ADD = mybir.AluOpType.mult, mybir.AluOpType.add
ACT = mybir.ActivationFunctionType


def tile_thinkerdecoderlayer_kernel(tc, base, x, gain, w1, w2, offs, out):
    nc = tc.nc
    with (
        tc.tile_pool(name="held", bufs=1) as held,
        tc.psum_pool(name="psum", bufs=1) as psum,
    ):
        offsets = held.tile([P, N // 16], U16, name="offsets")
        x_sb = [held.tile([P, N], F32, name=f"x{c}") for c in range(CB)]
        gain_sb = [held.tile([P, 1], F32, name=f"gain{c}") for c in range(CB)]
        w1_sb = [held.tile([P, I], BF16, name=f"w1_{c}") for c in range(CB)]
        w2_sb = [held.tile([P, C], BF16, name=f"w2_{e}") for e in range(EB)]
        window = [held.tile([P, S], F32, name=f"window{c}") for c in range(CB)]

        for c in range(CB):
            nc.sync.dma_start(x_sb[c][:], x[c * P : (c + 1) * P, :])
        for c in range(CB):
            nc.scalar.dma_start(gain_sb[c][:], gain[c * P : (c + 1) * P, :])
        for c in range(CB):
            nc.scalar.dma_start(w1_sb[c][:], w1[c * P : (c + 1) * P, :])
        for e in range(EB):
            nc.sync.dma_start(w2_sb[e][:], w2[e * P : (e + 1) * P, :])
        nc.sync.dma_start(offsets[:], offs)
        for c in range(CB):
            nc.sync.dma_start(window[c][:], base[c * P : (c + 1) * P, :])

        averager = held.tile([P, P], F32, name="averager")
        nc.vector.memset(averager[:], 1.0 / C)

        unread = psum.tile([WARM_COLUMNS, P], F32, name="unread")
        for i in range(WARM_MATMULS):
            nc.tensor.matmul(unread[:], averager[:, 0:WARM_COLUMNS], averager[:], start=True, stop=True)

        mean_sq = psum.tile([P, N], F32, name="mean_sq")
        for c in range(CB):
            x_sq = held.tile([P, N], F32, name=f"x_sq{c}")
            nc.vector.tensor_tensor(x_sq[:], x_sb[c][:], x_sb[c][:], MULT)
            nc.tensor.matmul(mean_sq[:], averager[:], x_sq[:], start=(c == 0), stop=(c == CB - 1))
        r = held.tile([P, N], F32, name="r")
        nc.scalar.activation(r[:], mean_sq[:], ACT.Abs_reciprocal_sqrt, bias=EPS)

        h = [held.tile([P, N], BF16, name=f"h{c}") for c in range(CB)]
        for c in range(CB):
            nc.vector.scalar_tensor_tensor(h[c][:], x_sb[c][:], gain_sb[c][:], r[:], MULT, MULT)

        pre = [psum.tile([P, N], F32, name=f"pre{e}") for e in range(EB)]
        for c in range(CB):
            for e in range(EB):
                nc.tensor.matmul(
                    pre[e][:], w1_sb[c][:, e * P : (e + 1) * P], h[c][:],
                    start=(c == 0), stop=(c == CB - 1),
                )

        y = [psum.tile([P, N], F32, name=f"y{c}") for c in range(CB)]
        u = [held.tile([P, N], BF16, name=f"u{e}") for e in range(EB)]
        for e in range(EB):
            nc.scalar.activation(u[e][:], pre[e][:], ACT.Silu)
        for c in range(CB):
            for e in range(EB):
                nc.tensor.matmul(
                    y[c][:], w2_sb[e][:, c * P : (c + 1) * P], u[e][:],
                    start=(e == 0), stop=(e == EB - 1),
                )

        for c in range(CB):
            y_sb = held.tile([P, N], F32, name=f"y_sb{c}")
            if c == 0:
                nc.vector.tensor_copy(y_sb[:], y[c][:])
            else:
                nc.scalar.copy(y_sb[:], y[c][:])
            nc.vector.tensor_tensor(window[c][:].indirect(offsets[:]), x_sb[c][:], y_sb[:], ADD)
            store = nc.scalar if c % 2 == 0 else nc.sync
            store.dma_start(out[c * P : (c + 1) * P, :], window[c][:])
